import numpy as np
import ml_dtypes


def mxq(x, axis, fmt="e4m3"):
    dtype, down = {"e4m3": (ml_dtypes.float8_e4m3fn, 7), "e5m2": (ml_dtypes.float8_e5m2, 14)}[fmt]
    v = np.moveaxis(np.asarray(x, np.float32).astype(ml_dtypes.bfloat16).astype(np.float64), axis, -1)
    blocks = v.reshape(v.shape[:-1] + (-1, 32))
    amax = np.abs(blocks).max(-1, keepdims=True)
    byte = np.maximum(np.where(amax > 0, np.frexp(amax)[1] - 1 + 127, 0) - down, 1)
    scale = np.exp2(byte - 127.0)
    codes = (blocks / scale).astype(np.float32).astype(dtype).astype(np.float64)
    return np.moveaxis((codes * scale).reshape(v.shape), -1, axis)


WIDE = False


def mx_kscale(k):
    if not WIDE:
        return np.ones(k)
    levels = np.array([20, -20, 10, -10, 0])
    a = np.random.permutation(np.resize(levels, k // 512 * 4)).reshape(k // 512, 4)
    idx = np.arange(k)
    return np.exp2(a[idx // 512, idx % 128 // 32])


BF16 = ml_dtypes.bfloat16


def bf(x):
    return np.asarray(x, np.float32).astype(BF16)


def f64(x):
    return np.asarray(x).astype(np.float64)


B, D, L0, L1, L2 = 4096, 512, 32, 512, 1024
KC = L1 + D
LN_EPS = 1e-5


def log_softmax(v):
    sh = v - v.max(-1, keepdims=True)
    return sh - np.log(np.exp(sh).sum(-1, keepdims=True))


def setup_inputs():
    s = mx_kscale(B)[:, None]
    W2 = bf(np.random.standard_normal((L2, KC)) * 1.5 / np.sqrt(KC))
    m0 = bf(np.random.standard_normal((B, L1)) * 3.0)
    x0 = bf(np.random.standard_normal((B, D)))
    b2 = bf(np.random.standard_normal(L2) * 0.5)
    g = bf(np.random.standard_normal((B, L2)) * np.exp2(np.random.randint(-12, 1, (B, 1))) * 0.25 / s)
    h = np.maximum(f64(m0), 0.0)
    mu = h.mean(-1, keepdims=True)
    rstd = 1.0 / np.sqrt(h.var(-1, keepdims=True) + LN_EPS)
    c = np.concatenate([(h - mu) * rstd, f64(x0)], axis=1)
    li = c @ f64(W2).T + f64(b2)
    p = np.exp(log_softmax(li))
    return {"mid_logits": bf(f64(m0) * s), "x": bf(f64(x0) * s), "W2": W2, "b2": b2,
            "rstd": np.asarray(rstd, np.float32), "p": np.asarray(p, np.float32), "grad_out": g}


def reference(mid_logits, x, W2, b2, rstd, p, grad_out):
    h = np.maximum(f64(mid_logits), 0.0)
    hn = (h - h.mean(-1, keepdims=True)) * f64(rstd)
    c = np.concatenate([hn, f64(x)], axis=1)
    g = f64(grad_out)
    dli = g - f64(p) * g.sum(-1, keepdims=True)
    return mxq(dli, 0, "e5m2").T @ mxq(c, 0, "e4m3")

@@ -1,0 +1,158 @@
+from contextlib import ExitStack
+
+import concourse.mybir as mybir
+
+F32 = mybir.dt.float32
+BF16 = mybir.dt.bfloat16
+U32 = mybir.dt.uint32
+U8 = mybir.dt.uint8
+E4M3_X4 = mybir.dt.float8_e4m3fn_x4
+E5M2_X4 = mybir.dt.float8_e5m2_x4
+ALU = mybir.AluOpType
+ACT = mybir.ActivationFunctionType
+
+P = 128
+PACK = 4
+TOKENS = 4096
+PASSES = TOKENS // (P * PACK)
+D_HN = 512
+D_X = 512
+KC = D_HN + D_X
+L2 = 1024
+M_TILE = 128
+N_TILE = 512
+N_TILES = KC // N_TILE
+PSUM_BANKS = 8
+M_TILES = PSUM_BANKS // N_TILES
+ROUND_COLS = M_TILES * M_TILE
+ROUNDS = L2 // ROUND_COLS
+RUN = 4
+
+FLOPS = 2 * L2 * KC * TOKENS
+BYTES = TOKENS * (2 * D_HN + 2 * D_X + 4 + 4 * L2 + 2 * L2) + 4 * L2 * KC
+
+
+def regroup(copy, grouped, rows):
+    copy(
+        out=grouped.rearrange("q (b i) t -> q b t i", i=RUN),
+        in_=rows.rearrange("q t (b i) -> q b t i", i=RUN),
+    )
+
+
+def tile_bhcn_awx_pa_t_v_kernel(tc, mid_logits, x, W2, b2, rstd, p, grad_out, out):
+    nc = tc.nc
+
+    mid_v = mid_logits.rearrange("(c q t) w -> c q t w", q=P, t=PACK)
+    x_v = x.rearrange("(c q t) w -> c q t w", q=P, t=PACK)
+    p_v = p.rearrange("(c q t) w -> c q t w", q=P, t=PACK)
+    g_v = grad_out.rearrange("(c q t) w -> c q t w", q=P, t=PACK)
+    rstd_v = rstd.rearrange("(c q t) o -> q c (t o)", q=P, t=PACK)
+
+    with ExitStack() as ctx:
+        keep = ctx.enter_context(tc.tile_pool(name="keep", bufs=1))
+        p_pool = ctx.enter_context(tc.tile_pool(name="p_pool", bufs=4))
+        c_in = ctx.enter_context(tc.tile_pool(name="c_in", bufs=3))
+        small = ctx.enter_context(tc.tile_pool(name="small", bufs=3))
+        grouped_pool = ctx.enter_context(tc.tile_pool(name="grouped_pool", bufs=2))
+        d_pool = ctx.enter_context(tc.tile_pool(name="d_pool", bufs=4))
+        out_pool = ctx.enter_context(tc.tile_pool(name="out_pool", bufs=2))
+        psum = ctx.enter_context(tc.psum_pool(name="psum", bufs=1))
+
+        rstd_sb = keep.tile([P, PASSES, PACK], F32)
+        g_sb = [keep.tile([P, PACK, L2], BF16, name="g_sb%d" % c) for c in range(PASSES)]
+        neg_s = [keep.tile([P, PACK], F32, name="neg_s%d" % c) for c in range(PASSES)]
+        c_codes = [keep.tile([P, KC], U32, name="c_codes%d" % c, align_bytes=64) for c in range(PASSES)]
+        c_scales = [keep.tile([P, KC], U8, name="c_scales%d" % c, align_bytes=64) for c in range(PASSES)]
+
+        nc.scalar.dma_start(out=rstd_sb[:], in_=rstd_v)
+
+        for r in range(ROUNDS):
+            d_cols = slice(r * ROUND_COLS, (r + 1) * ROUND_COLS)
+            acc = [
+                [psum.tile([P, N_TILE], F32, name="acc%d%d" % (m, n)) for n in range(N_TILES)]
+                for m in range(M_TILES)
+            ]
+
+            for c in range(PASSES):
+                p_sb = p_pool.tile([P, PACK, ROUND_COLS], F32)
+
+                if r == 0:
+                    mid_sb = c_in.tile([P, PACK, D_HN], BF16)
+                    x_sb = c_in.tile([P, PACK, D_X], BF16)
+                    nc.sync.dma_start(out=g_sb[c][:], in_=g_v[c])
+                    nc.sync.dma_start(out=mid_sb[:], in_=mid_v[c])
+                    nc.sync.dma_start(out=p_sb[:], in_=p_v[c, :, :, d_cols])
+                    nc.sync.dma_start(out=x_sb[:], in_=x_v[c])
+
+                    s = small.tile([P, PACK], F32)
+                    h_sum = small.tile([P, PACK], F32)
+                    for t in range(PACK):
+                        nc.scalar.activation(
+                            out=g_sb[c][:, t, :], in_=g_sb[c][:, t, :], func=ACT.Copy,
+                            accum_out=s[:, t : t + 1],
+                        )
+                    for t in range(PACK):
+                        nc.scalar.activation(
+                            out=mid_sb[:, t, :], in_=mid_sb[:, t, :], func=ACT.Relu,
+                            accum_out=h_sum[:, t : t + 1],
+                        )
+                    mu = small.tile([P, PACK], F32)
+                    nc.vector.tensor_scalar(
+                        out=neg_s[c][:], in0=s[:], scalar1=-1.0, scalar2=None, op0=ALU.mult
+                    )
+                    nc.vector.tensor_scalar(
+                        out=mu[:], in0=h_sum[:], scalar1=1.0 / D_HN, scalar2=None, op0=ALU.mult
+                    )
+
+                    for t in range(PACK):
+                        nc.vector.tensor_scalar(
+                            out=mid_sb[:, t, :], in0=mid_sb[:, t, :],
+                            scalar1=mu[:, t : t + 1], scalar2=rstd_sb[:, c, t : t + 1],
+                            op0=ALU.subtract, op1=ALU.mult,
+                        )
+                    c_grouped = grouped_pool.tile([P, KC, PACK], BF16, align_bytes=64)
+                    regroup(nc.vector.tensor_copy, c_grouped[:, 0:D_HN, :], mid_sb[:])
+                    regroup(nc.vector.tensor_copy, c_grouped[:, D_HN:KC, :], x_sb[:])
+                    nc.vector.quantize_mx(
+                        out=c_codes[c][:].bitcast(E4M3_X4),
+                        scales=c_scales[c][:],
+                        in_=c_grouped[:].rearrange("q w t -> q (w t)"),
+                    )
+                else:
+                    nc.sync.dma_start(out=p_sb[:], in_=p_v[c, :, :, d_cols])
+
+                for t in range(PACK):
+                    nc.vector.scalar_tensor_tensor(
+                        out=g_sb[c][:, t, d_cols], in0=p_sb[:, t, :], scalar=neg_s[c][:, t : t + 1],
+                        in1=g_sb[c][:, t, d_cols], op0=ALU.mult, op1=ALU.add,
+                    )
+                d_grouped = grouped_pool.tile([P, ROUND_COLS, PACK], BF16, align_bytes=64)
+                regroup(nc.vector.tensor_copy if r == 0 else nc.scalar.copy, d_grouped[:], g_sb[c][:, :, d_cols])
+                d_codes = d_pool.tile([P, ROUND_COLS], U32, align_bytes=64)
+                d_scales = d_pool.tile([P, ROUND_COLS], U8, align_bytes=64)
+                nc.vector.quantize_mx(
+                    out=d_codes[:].bitcast(E5M2_X4),
+                    scales=d_scales[:],
+                    in_=d_grouped[:].rearrange("q w t -> q (w t)"),
+                )
+
+                for m in range(M_TILES):
+                    m_cols = slice(m * M_TILE, (m + 1) * M_TILE)
+                    for n in range(N_TILES):
+                        n_cols = slice(n * N_TILE, (n + 1) * N_TILE)
+                        nc.tensor.matmul_mx(
+                            out=acc[m][n][:],
+                            lhsT=d_codes[:, m_cols].bitcast(E5M2_X4),
+                            lhsT_scale=d_scales[:, m_cols],
+                            rhs=c_codes[c][:, n_cols].bitcast(E4M3_X4),
+                            rhs_scale=c_scales[c][:, n_cols],
+                            start=(c == 0),
+                            stop=(c == PASSES - 1),
+                        )
+
+            for m in range(M_TILES):
+                row0 = r * ROUND_COLS + m * M_TILE
+                staged = out_pool.tile([P, KC], F32)
+                nc.scalar.copy(out=staged[:, 0:N_TILE], in_=acc[m][0][:])
+                nc.vector.tensor_copy(out=staged[:, N_TILE:KC], in_=acc[m][1][:])
+                nc.sync.dma_start(out=out[row0 : row0 + M_TILE, :], in_=staged[:])

@@ -26,6 +26,8 @@ PSUM_BANKS = 8
 M_TILES = PSUM_BANKS // N_TILES
 ROUND_COLS = M_TILES * M_TILE
 ROUNDS = L2 // ROUND_COLS
+CHUNK_TILES = 2
+CHUNK_COLS = CHUNK_TILES * M_TILE
 RUN = 4
 
 FLOPS = 2 * L2 * KC * TOKENS
@@ -53,9 +55,9 @@ def tile_bhcn_awx_pa_t_v_kernel(tc, mid_logits, x, W2, b2, rstd, p, grad_out, ou
         p_pool = ctx.enter_context(tc.tile_pool(name="p_pool", bufs=4))
         c_in = ctx.enter_context(tc.tile_pool(name="c_in", bufs=3))
         small = ctx.enter_context(tc.tile_pool(name="small", bufs=3))
-        grouped_pool = ctx.enter_context(tc.tile_pool(name="grouped_pool", bufs=2))
-        d_pool = ctx.enter_context(tc.tile_pool(name="d_pool", bufs=4))
-        out_pool = ctx.enter_context(tc.tile_pool(name="out_pool", bufs=2))
+        grouped_pool = ctx.enter_context(tc.tile_pool(name="grouped_pool", bufs=3))
+        d_pool = ctx.enter_context(tc.tile_pool(name="d_pool", bufs=6))
+        out_pool = ctx.enter_context(tc.tile_pool(name="out_pool", bufs=M_TILES))
         psum = ctx.enter_context(tc.psum_pool(name="psum", bufs=1))
 
         rstd_sb = keep.tile([P, PASSES, PACK], F32)
@@ -79,27 +81,23 @@ def tile_bhcn_awx_pa_t_v_kernel(tc, mid_logits, x, W2, b2, rstd, p, grad_out, ou
                 if r == 0:
                     mid_sb = c_in.tile([P, PACK, D_HN], BF16)
                     x_sb = c_in.tile([P, PACK, D_X], BF16)
-                    nc.sync.dma_start(out=g_sb[c][:], in_=g_v[c])
                     nc.sync.dma_start(out=mid_sb[:], in_=mid_v[c])
-                    nc.sync.dma_start(out=p_sb[:], in_=p_v[c, :, :, d_cols])
                     nc.sync.dma_start(out=x_sb[:], in_=x_v[c])
+                    nc.sync.dma_start(out=g_sb[c][:], in_=g_v[c])
+                    nc.sync.dma_start(out=p_sb[:], in_=p_v[c, :, :, d_cols])
 
-                    s = small.tile([P, PACK], F32)
                     h_sum = small.tile([P, PACK], F32)
-                    for t in range(PACK):
-                        nc.scalar.activation(
-                            out=g_sb[c][:, t, :], in_=g_sb[c][:, t, :], func=ACT.Copy,
-                            accum_out=s[:, t : t + 1],
-                        )
                     for t in range(PACK):
                         nc.scalar.activation(
                             out=mid_sb[:, t, :], in_=mid_sb[:, t, :], func=ACT.Relu,
                             accum_out=h_sum[:, t : t + 1],
                         )
+                    for t in range(PACK):
+                        nc.scalar.activation(
+                            out=g_sb[c][:, t, :], in_=g_sb[c][:, t, :], func=ACT.Copy, scale=-1.0,
+                            accum_out=neg_s[c][:, t : t + 1],
+                        )
                     mu = small.tile([P, PACK], F32)
-                    nc.vector.tensor_scalar(
-                        out=neg_s[c][:], in0=s[:], scalar1=-1.0, scalar2=None, op0=ALU.mult
-                    )
                     nc.vector.tensor_scalar(
                         out=mu[:], in0=h_sum[:], scalar1=1.0 / D_HN, scalar2=None, op0=ALU.mult
                     )
@@ -124,35 +122,41 @@ def tile_bhcn_awx_pa_t_v_kernel(tc, mid_logits, x, W2, b2, rstd, p, grad_out, ou
                 for t in range(PACK):
                     nc.vector.scalar_tensor_tensor(
                         out=g_sb[c][:, t, d_cols], in0=p_sb[:, t, :], scalar=neg_s[c][:, t : t + 1],
-                        in1=g_sb[c][:, t, d_cols], op0=ALU.mult, op1=ALU.add,
+                        in1=g_sb[c][:, t, d_cols], op0=ALU.mult, op1=ALU.subtract,
                     )
-                d_grouped = grouped_pool.tile([P, ROUND_COLS, PACK], BF16, align_bytes=64)
-                regroup(nc.vector.tensor_copy if r == 0 else nc.scalar.copy, d_grouped[:], g_sb[c][:, :, d_cols])
-                d_codes = d_pool.tile([P, ROUND_COLS], U32, align_bytes=64)
-                d_scales = d_pool.tile([P, ROUND_COLS], U8, align_bytes=64)
-                nc.vector.quantize_mx(
-                    out=d_codes[:].bitcast(E5M2_X4),
-                    scales=d_scales[:],
-                    in_=d_grouped[:].rearrange("q w t -> q (w t)"),
-                )
-
-                for m in range(M_TILES):
-                    m_cols = slice(m * M_TILE, (m + 1) * M_TILE)
-                    for n in range(N_TILES):
-                        n_cols = slice(n * N_TILE, (n + 1) * N_TILE)
-                        nc.tensor.matmul_mx(
-                            out=acc[m][n][:],
-                            lhsT=d_codes[:, m_cols].bitcast(E5M2_X4),
-                            lhsT_scale=d_scales[:, m_cols],
-                            rhs=c_codes[c][:, n_cols].bitcast(E4M3_X4),
-                            rhs_scale=c_scales[c][:, n_cols],
-                            start=(c == 0),
-                            stop=(c == PASSES - 1),
-                        )
+                for m0 in range(0, M_TILES, CHUNK_TILES):
+                    col0 = r * ROUND_COLS + m0 * M_TILE
+                    d_grouped = grouped_pool.tile([P, CHUNK_COLS, PACK], BF16, align_bytes=64)
+                    regroup(
+                        nc.vector.tensor_copy if r == 0 else nc.scalar.copy,
+                        d_grouped[:],
+                        g_sb[c][:, :, col0 : col0 + CHUNK_COLS],
+                    )
+                    d_codes = d_pool.tile([P, CHUNK_COLS], U32, align_bytes=64)
+                    d_scales = d_pool.tile([P, CHUNK_COLS], U8, align_bytes=64)
+                    nc.vector.quantize_mx(
+                        out=d_codes[:].bitcast(E5M2_X4),
+                        scales=d_scales[:],
+                        in_=d_grouped[:].rearrange("q w t -> q (w t)"),
+                    )
+                    for i in range(CHUNK_TILES):
+                        m_cols = slice(i * M_TILE, (i + 1) * M_TILE)
+                        for n in range(N_TILES):
+                            n_cols = slice(n * N_TILE, (n + 1) * N_TILE)
+                            nc.tensor.matmul_mx(
+                                out=acc[m0 + i][n][:],
+                                lhsT=d_codes[:, m_cols].bitcast(E5M2_X4),
+                                lhsT_scale=d_scales[:, m_cols],
+                                rhs=c_codes[c][:, n_cols].bitcast(E4M3_X4),
+                                rhs_scale=c_scales[c][:, n_cols],
+                                start=(c == 0),
+                                stop=(c == PASSES - 1),
+                            )
 
             for m in range(M_TILES):
                 row0 = r * ROUND_COLS + m * M_TILE
                 staged = out_pool.tile([P, KC], F32)
                 nc.scalar.copy(out=staged[:, 0:N_TILE], in_=acc[m][0][:])
-                nc.vector.tensor_copy(out=staged[:, N_TILE:KC], in_=acc[m][1][:])
+                second_copy = nc.vector.tensor_copy if r == ROUNDS - 1 else nc.scalar.copy
+                second_copy(out=staged[:, N_TILE:KC], in_=acc[m][1][:])
                 nc.sync.dma_start(out=out[row0 : row0 + M_TILE, :], in_=staged[:])

@@ -28,17 +28,19 @@ ROUND_COLS = M_TILES * M_TILE
 ROUNDS = L2 // ROUND_COLS
 CHUNK_TILES = 2
 CHUNK_COLS = CHUNK_TILES * M_TILE
+CHUNKS = M_TILES // CHUNK_TILES
 RUN = 4
 
 FLOPS = 2 * L2 * KC * TOKENS
 BYTES = TOKENS * (2 * D_HN + 2 * D_X + 4 + 4 * L2 + 2 * L2) + 4 * L2 * KC
 
 
-def regroup(copy, grouped, rows):
-    copy(
-        out=grouped.rearrange("q (b i) t -> q b t i", i=RUN),
-        in_=rows.rearrange("q t (b i) -> q b t i", i=RUN),
-    )
+def as_rows(rows):
+    return rows.rearrange("q t (b i) -> q b t i", i=RUN)
+
+
+def as_grouped(grouped):
+    return grouped.rearrange("q (b i) t -> q b t i", i=RUN)
 
 
 def tile_bhcn_awx_pa_t_v_kernel(tc, mid_logits, x, W2, b2, rstd, p, grad_out, out):
@@ -52,11 +54,12 @@ def tile_bhcn_awx_pa_t_v_kernel(tc, mid_logits, x, W2, b2, rstd, p, grad_out, ou
 
     with ExitStack() as ctx:
         keep = ctx.enter_context(tc.tile_pool(name="keep", bufs=1))
-        p_pool = ctx.enter_context(tc.tile_pool(name="p_pool", bufs=4))
+        p_pool = ctx.enter_context(tc.tile_pool(name="p_pool", bufs=6))
         c_in = ctx.enter_context(tc.tile_pool(name="c_in", bufs=3))
         small = ctx.enter_context(tc.tile_pool(name="small", bufs=3))
-        grouped_pool = ctx.enter_context(tc.tile_pool(name="grouped_pool", bufs=3))
-        d_pool = ctx.enter_context(tc.tile_pool(name="d_pool", bufs=6))
+        c_grouped_pool = ctx.enter_context(tc.tile_pool(name="c_grouped_pool", bufs=2))
+        d_grouped_pool = ctx.enter_context(tc.tile_pool(name="d_grouped_pool", bufs=2 * CHUNKS))
+        d_pool = ctx.enter_context(tc.tile_pool(name="d_pool", bufs=3 * CHUNKS))
         out_pool = ctx.enter_context(tc.tile_pool(name="out_pool", bufs=M_TILES))
         psum = ctx.enter_context(tc.psum_pool(name="psum", bufs=1))
 
@@ -84,8 +87,9 @@ def tile_bhcn_awx_pa_t_v_kernel(tc, mid_logits, x, W2, b2, rstd, p, grad_out, ou
                     nc.sync.dma_start(out=mid_sb[:], in_=mid_v[c])
                     nc.sync.dma_start(out=x_sb[:], in_=x_v[c])
                     nc.sync.dma_start(out=g_sb[c][:], in_=g_v[c])
-                    nc.sync.dma_start(out=p_sb[:], in_=p_v[c, :, :, d_cols])
+                nc.sync.dma_start(out=p_sb[:], in_=p_v[c, :, :, d_cols])
 
+                if r == 0:
                     h_sum = small.tile([P, PACK], F32)
                     for t in range(PACK):
                         nc.scalar.activation(
@@ -102,49 +106,70 @@ def tile_bhcn_awx_pa_t_v_kernel(tc, mid_logits, x, W2, b2, rstd, p, grad_out, ou
                         out=mu[:], in0=h_sum[:], scalar1=1.0 / D_HN, scalar2=None, op0=ALU.mult
                     )
 
+                for t in range(PACK):
+                    if r == 0:
+                        nc.vector.scalar_tensor_tensor(
+                            out=g_sb[c][:, t, d_cols], in0=p_sb[:, t, :], scalar=neg_s[c][:, t : t + 1],
+                            in1=g_sb[c][:, t, d_cols], op0=ALU.mult, op1=ALU.subtract,
+                        )
+                    else:
+                        nc.scalar.activation(
+                            out=p_sb[:, t, :], in_=p_sb[:, t, :], func=ACT.Copy,
+                            scale=neg_s[c][:, t : t + 1],
+                        )
+
+                if r == 0:
                     for t in range(PACK):
                         nc.vector.tensor_scalar(
                             out=mid_sb[:, t, :], in0=mid_sb[:, t, :],
                             scalar1=mu[:, t : t + 1], scalar2=rstd_sb[:, c, t : t + 1],
                             op0=ALU.subtract, op1=ALU.mult,
                         )
-                    c_grouped = grouped_pool.tile([P, KC, PACK], BF16, align_bytes=64)
-                    regroup(nc.vector.tensor_copy, c_grouped[:, 0:D_HN, :], mid_sb[:])
-                    regroup(nc.vector.tensor_copy, c_grouped[:, D_HN:KC, :], x_sb[:])
+                    c_grouped = c_grouped_pool.tile([P, KC, PACK], BF16, align_bytes=64)
+                    nc.vector.tensor_copy(out=as_grouped(c_grouped[:, D_HN:KC, :]), in_=as_rows(x_sb[:]))
+                    nc.vector.tensor_copy(out=as_grouped(c_grouped[:, 0:D_HN, :]), in_=as_rows(mid_sb[:]))
+
+                d_grouped = []
+                for k in range(CHUNKS):
+                    p_col0 = k * CHUNK_COLS
+                    g_col0 = r * ROUND_COLS + p_col0
+                    d_grouped.append(
+                        d_grouped_pool.tile([P, CHUNK_COLS, PACK], BF16, name="d_grouped", align_bytes=64)
+                    )
+                    if r == 0:
+                        nc.vector.tensor_copy(
+                            out=as_grouped(d_grouped[k][:]),
+                            in_=as_rows(g_sb[c][:, :, g_col0 : g_col0 + CHUNK_COLS]),
+                        )
+                    else:
+                        nc.vector.tensor_tensor(
+                            out=as_grouped(d_grouped[k][:]),
+                            in0=as_rows(p_sb[:, :, p_col0 : p_col0 + CHUNK_COLS]),
+                            in1=as_rows(g_sb[c][:, :, g_col0 : g_col0 + CHUNK_COLS]),
+                            op=ALU.subtract,
+                        )
+
+                if r == 0:
                     nc.vector.quantize_mx(
                         out=c_codes[c][:].bitcast(E4M3_X4),
                         scales=c_scales[c][:],
                         in_=c_grouped[:].rearrange("q w t -> q (w t)"),
                     )
-                else:
-                    nc.sync.dma_start(out=p_sb[:], in_=p_v[c, :, :, d_cols])
 
-                for t in range(PACK):
-                    nc.vector.scalar_tensor_tensor(
-                        out=g_sb[c][:, t, d_cols], in0=p_sb[:, t, :], scalar=neg_s[c][:, t : t + 1],
-                        in1=g_sb[c][:, t, d_cols], op0=ALU.mult, op1=ALU.subtract,
-                    )
-                for m0 in range(0, M_TILES, CHUNK_TILES):
-                    col0 = r * ROUND_COLS + m0 * M_TILE
-                    d_grouped = grouped_pool.tile([P, CHUNK_COLS, PACK], BF16, align_bytes=64)
-                    regroup(
-                        nc.vector.tensor_copy if r == 0 else nc.scalar.copy,
-                        d_grouped[:],
-                        g_sb[c][:, :, col0 : col0 + CHUNK_COLS],
-                    )
+                for k in range(CHUNKS):
                     d_codes = d_pool.tile([P, CHUNK_COLS], U32, align_bytes=64)
                     d_scales = d_pool.tile([P, CHUNK_COLS], U8, align_bytes=64)
                     nc.vector.quantize_mx(
                         out=d_codes[:].bitcast(E5M2_X4),
                         scales=d_scales[:],
-                        in_=d_grouped[:].rearrange("q w t -> q (w t)"),
+                        in_=d_grouped[k][:].rearrange("q w t -> q (w t)"),
                     )
                     for i in range(CHUNK_TILES):
                         m_cols = slice(i * M_TILE, (i + 1) * M_TILE)
                         for n in range(N_TILES):
                             n_cols = slice(n * N_TILE, (n + 1) * N_TILE)
                             nc.tensor.matmul_mx(
-                                out=acc[m0 + i][n][:],
+                                out=acc[k * CHUNK_TILES + i][n][:],
                                 lhsT=d_codes[:, m_cols].bitcast(E5M2_X4),
                                 lhsT_scale=d_scales[:, m_cols],
                                 rhs=c_codes[c][:, n_cols].bitcast(E4M3_X4),

@@ -1,6 +1,7 @@
 from contextlib import ExitStack
 
 import concourse.mybir as mybir
+from concourse.masks import make_identity
 
 F32 = mybir.dt.float32
 BF16 = mybir.dt.bfloat16
@@ -10,6 +11,7 @@ E4M3_X4 = mybir.dt.float8_e4m3fn_x4
 E5M2_X4 = mybir.dt.float8_e5m2_x4
 ALU = mybir.AluOpType
 ACT = mybir.ActivationFunctionType
+AX = mybir.AxisListType
 
 P = 128
 PACK = 4
@@ -29,6 +31,8 @@ ROUNDS = L2 // ROUND_COLS
 CHUNK_TILES = 2
 CHUNK_COLS = CHUNK_TILES * M_TILE
 CHUNKS = M_TILES // CHUNK_TILES
+FOLD_W = 32
+FOLD_COLS = 800
 RUN = 4
 
 FLOPS = 2 * L2 * KC * TOKENS
@@ -62,14 +66,74 @@ def tile_bhcn_awx_pa_t_v_kernel(tc, mid_logits, x, W2, b2, rstd, p, grad_out, ou
         d_pool = ctx.enter_context(tc.tile_pool(name="d_pool", bufs=3 * CHUNKS))
         out_pool = ctx.enter_context(tc.tile_pool(name="out_pool", bufs=M_TILES))
         psum = ctx.enter_context(tc.psum_pool(name="psum", bufs=1))
+        ctx.enter_context(tc.manual_schedule(engines={mybir.EngineType.SP}))
 
         rstd_sb = keep.tile([P, PASSES, PACK], F32)
+        ident = keep.tile([P, P], BF16)
         g_sb = [keep.tile([P, PACK, L2], BF16, name="g_sb%d" % c) for c in range(PASSES)]
-        neg_s = [keep.tile([P, PACK], F32, name="neg_s%d" % c) for c in range(PASSES)]
+        row_sum = [keep.tile([P, PACK], F32, name="row_sum%d" % c) for c in range(PASSES)]
         c_codes = [keep.tile([P, KC], U32, name="c_codes%d" % c, align_bytes=64) for c in range(PASSES)]
         c_scales = [keep.tile([P, KC], U8, name="c_scales%d" % c, align_bytes=64) for c in range(PASSES)]
 
         nc.scalar.dma_start(out=rstd_sb[:], in_=rstd_v)
+        make_identity(nc, ident[:])
+
+        def quantise_c(c, c_grouped):
+            nc.vector.quantize_mx(
+                out=c_codes[c][:].bitcast(E4M3_X4),
+                scales=c_scales[c][:],
+                in_=c_grouped[:].rearrange("q w t -> q (w t)"),
+            )
+
+        waiting = None
+        for c in range(PASSES):
+            mid_sb = c_in.tile([P, PACK, D_HN], BF16)
+            x_sb = c_in.tile([P, PACK, D_X], BF16)
+            nc.sync.dma_start(out=mid_sb[:], in_=mid_v[c])
+            nc.sync.dma_start(out=x_sb[:], in_=x_v[c])
+            nc.sync.dma_start(out=g_sb[c][:], in_=g_v[c])
+
+            h_sum = small.tile([P, PACK], F32)
+            for t in range(PACK):
+                nc.scalar.activation(
+                    out=mid_sb[:, t, :], in_=mid_sb[:, t, :], func=ACT.Relu,
+                    accum_out=h_sum[:, t : t + 1],
+                )
+            mu = small.tile([P, PACK], F32)
+            nc.scalar.mul(mu[:], h_sum[:], 1.0 / D_HN)
+            rest_sum = small.tile([P, PACK], F32)
+            unused = small.tile([P, L2 - FOLD_COLS], BF16)
+            for t in range(PACK):
+                nc.scalar.activation(
+                    out=unused[:], in_=g_sb[c][:, t, FOLD_COLS:L2], func=ACT.Copy,
+                    accum_out=rest_sum[:, t : t + 1],
+                )
+
+            bank = psum.tile([P, N_TILE], F32, name="acc%d%d" % (c // N_TILES, c % N_TILES))
+            fold = bank[:, 0 : PACK * FOLD_W].rearrange("q (t i) -> q t i", t=PACK)
+            folds = FOLD_COLS // FOLD_W
+            for j in range(folds):
+                nc.tensor.matmul(
+                    out=fold, lhsT=ident[:], rhs=g_sb[c][:, :, j * FOLD_W : (j + 1) * FOLD_W],
+                    start=(j == 0), stop=(j == folds - 1),
+                )
+
+            c_grouped = c_grouped_pool.tile([P, KC, PACK], BF16, align_bytes=64)
+            nc.vector.tensor_copy(out=as_grouped(c_grouped[:, D_HN:KC, :]), in_=as_rows(x_sb[:]))
+            if waiting is not None:
+                quantise_c(*waiting)
+            for t in range(PACK):
+                nc.vector.tensor_scalar(
+                    out=mid_sb[:, t, :], in0=mid_sb[:, t, :],
+                    scalar1=mu[:, t : t + 1], scalar2=rstd_sb[:, c, t : t + 1],
+                    op0=ALU.subtract, op1=ALU.mult,
+                )
+            nc.vector.tensor_copy(out=as_grouped(c_grouped[:, 0:D_HN, :]), in_=as_rows(mid_sb[:]))
+            waiting = (c, c_grouped)
+            fold_sum = small.tile([P, PACK], F32)
+            nc.vector.tensor_reduce(out=fold_sum[:], in_=fold, axis=AX.X, op=ALU.add)
+            nc.gpsimd.tensor_tensor(out=row_sum[c][:], in0=fold_sum[:], in1=rest_sum[:], op=ALU.add)
+        quantise_c(*waiting)
 
         for r in range(ROUNDS):
             d_cols = slice(r * ROUND_COLS, (r + 1) * ROUND_COLS)
@@ -80,54 +144,13 @@ def tile_bhcn_awx_pa_t_v_kernel(tc, mid_logits, x, W2, b2, rstd, p, grad_out, ou
 
             for c in range(PASSES):
                 p_sb = p_pool.tile([P, PACK, ROUND_COLS], F32)
-
-                if r == 0:
-                    mid_sb = c_in.tile([P, PACK, D_HN], BF16)
-                    x_sb = c_in.tile([P, PACK, D_X], BF16)
-                    nc.sync.dma_start(out=mid_sb[:], in_=mid_v[c])
-                    nc.sync.dma_start(out=x_sb[:], in_=x_v[c])
-                    nc.sync.dma_start(out=g_sb[c][:], in_=g_v[c])
                 nc.sync.dma_start(out=p_sb[:], in_=p_v[c, :, :, d_cols])
 
-                if r == 0:
-                    h_sum = small.tile([P, PACK], F32)
-                    for t in range(PACK):
-                        nc.scalar.activation(
-                            out=mid_sb[:, t, :], in_=mid_sb[:, t, :], func=ACT.Relu,
-                            accum_out=h_sum[:, t : t + 1],
-                        )
-                    for t in range(PACK):
-                        nc.scalar.activation(
-                            out=g_sb[c][:, t, :], in_=g_sb[c][:, t, :], func=ACT.Copy, scale=-1.0,
-                            accum_out=neg_s[c][:, t : t + 1],
-                        )
-                    mu = small.tile([P, PACK], F32)
-                    nc.vector.tensor_scalar(
-                        out=mu[:], in0=h_sum[:], scalar1=1.0 / D_HN, scalar2=None, op0=ALU.mult
-                    )
-
                 for t in range(PACK):
-                    if r == 0:
-                        nc.vector.scalar_tensor_tensor(
-                            out=g_sb[c][:, t, d_cols], in0=p_sb[:, t, :], scalar=neg_s[c][:, t : t + 1],
-                            in1=g_sb[c][:, t, d_cols], op0=ALU.mult, op1=ALU.subtract,
-                        )
-                    else:
-                        nc.scalar.activation(
-                            out=p_sb[:, t, :], in_=p_sb[:, t, :], func=ACT.Copy,
-                            scale=neg_s[c][:, t : t + 1],
-                        )
-
-                if r == 0:
-                    for t in range(PACK):
-                        nc.vector.tensor_scalar(
-                            out=mid_sb[:, t, :], in0=mid_sb[:, t, :],
-                            scalar1=mu[:, t : t + 1], scalar2=rstd_sb[:, c, t : t + 1],
-                            op0=ALU.subtract, op1=ALU.mult,
-                        )
-                    c_grouped = c_grouped_pool.tile([P, KC, PACK], BF16, align_bytes=64)
-                    nc.vector.tensor_copy(out=as_grouped(c_grouped[:, D_HN:KC, :]), in_=as_rows(x_sb[:]))
-                    nc.vector.tensor_copy(out=as_grouped(c_grouped[:, 0:D_HN, :]), in_=as_rows(mid_sb[:]))
+                    nc.scalar.activation(
+                        out=p_sb[:, t, :], in_=p_sb[:, t, :], func=ACT.Copy,
+                        scale=row_sum[c][:, t : t + 1],
+                    )
 
                 d_grouped = []
                 for k in range(CHUNKS):
@@ -136,24 +159,11 @@ def tile_bhcn_awx_pa_t_v_kernel(tc, mid_logits, x, W2, b2, rstd, p, grad_out, ou
                     d_grouped.append(
                         d_grouped_pool.tile([P, CHUNK_COLS, PACK], BF16, name="d_grouped", align_bytes=64)
                     )
-                    if r == 0:
-                        nc.vector.tensor_copy(
-                            out=as_grouped(d_grouped[k][:]),
-                            in_=as_rows(g_sb[c][:, :, g_col0 : g_col0 + CHUNK_COLS]),
-                        )
-                    else:
-                        nc.vector.tensor_tensor(
-                            out=as_grouped(d_grouped[k][:]),
-                            in0=as_rows(p_sb[:, :, p_col0 : p_col0 + CHUNK_COLS]),
-                            in1=as_rows(g_sb[c][:, :, g_col0 : g_col0 + CHUNK_COLS]),
-                            op=ALU.subtract,
-                        )
-
-                if r == 0:
-                    nc.vector.quantize_mx(
-                        out=c_codes[c][:].bitcast(E4M3_X4),
-                        scales=c_scales[c][:],
-                        in_=c_grouped[:].rearrange("q w t -> q (w t)"),
+                    nc.vector.tensor_tensor(
+                        out=as_grouped(d_grouped[k][:]),
+                        in0=as_rows(g_sb[c][:, :, g_col0 : g_col0 + CHUNK_COLS]),
+                        in1=as_rows(p_sb[:, :, p_col0 : p_col0 + CHUNK_COLS]),
+                        op=ALU.subtract,
                     )
 
                 for k in range(CHUNKS):
@@ -184,4 +194,4 @@ def tile_bhcn_awx_pa_t_v_kernel(tc, mid_logits, x, W2, b2, rstd, p, grad_out, ou
                 nc.scalar.copy(out=staged[:, 0:N_TILE], in_=acc[m][0][:])
                 second_copy = nc.vector.tensor_copy if r == ROUNDS - 1 else nc.scalar.copy
                 second_copy(out=staged[:, N_TILE:KC], in_=acc[m][1][:])
-                nc.sync.dma_start(out=out[row0 : row0 + M_TILE, :], in_=staged[:])
+                nc.scalar.dma_start(out=out[row0 : row0 + M_TILE, :], in_=staged[:])

@@ -33,6 +33,7 @@ CHUNK_COLS = CHUNK_TILES * M_TILE
 CHUNKS = M_TILES // CHUNK_TILES
 FOLD_W = 32
 FOLD_COLS = 800
+SCALAR_X_COLS = 128
 RUN = 4
 
 FLOPS = 2 * L2 * KC * TOKENS
@@ -89,8 +90,17 @@ def tile_bhcn_awx_pa_t_v_kernel(tc, mid_logits, x, W2, b2, rstd, p, grad_out, ou
         for c in range(PASSES):
             mid_sb = c_in.tile([P, PACK, D_HN], BF16)
             x_sb = c_in.tile([P, PACK, D_X], BF16)
-            nc.sync.dma_start(out=mid_sb[:], in_=mid_v[c])
-            nc.sync.dma_start(out=x_sb[:], in_=x_v[c])
+            x_pieces = 2 if c == 0 else 1
+            x_cols = D_X // x_pieces
+            if c == 0:
+                for i in range(x_pieces):
+                    for t in range(i * PACK // x_pieces, (i + 1) * PACK // x_pieces):
+                        nc.sync.dma_start(out=mid_sb[:, t, :], in_=mid_v[c, :, t, :])
+                    piece = slice(i * x_cols, (i + 1) * x_cols)
+                    nc.sync.dma_start(out=x_sb[:, :, piece], in_=x_v[c, :, :, piece])
+            else:
+                nc.sync.dma_start(out=mid_sb[:], in_=mid_v[c])
+                nc.sync.dma_start(out=x_sb[:], in_=x_v[c])
             nc.sync.dma_start(out=g_sb[c][:], in_=g_v[c])
 
             h_sum = small.tile([P, PACK], F32)
@@ -119,7 +129,16 @@ def tile_bhcn_awx_pa_t_v_kernel(tc, mid_logits, x, W2, b2, rstd, p, grad_out, ou
                 )
 
             c_grouped = c_grouped_pool.tile([P, KC, PACK], BF16, align_bytes=64)
-            nc.vector.tensor_copy(out=as_grouped(c_grouped[:, D_HN:KC, :]), in_=as_rows(x_sb[:]))
+            nc.scalar.copy(
+                out=as_grouped(c_grouped[:, KC - SCALAR_X_COLS : KC, :]),
+                in_=as_rows(x_sb[:, :, D_X - SCALAR_X_COLS : D_X]),
+            )
+            for i in range(x_pieces):
+                last = min((i + 1) * x_cols, D_X - SCALAR_X_COLS)
+                nc.vector.tensor_copy(
+                    out=as_grouped(c_grouped[:, D_HN + i * x_cols : D_HN + last, :]),
+                    in_=as_rows(x_sb[:, :, i * x_cols : last]),
+                )
             if waiting is not None:
                 quantise_c(*waiting)
             for t in range(PACK):

@@ -34,6 +34,12 @@ CHUNKS = M_TILES // CHUNK_TILES
 FOLD_W = 32
 FOLD_COLS = 800
 SCALAR_X_COLS = 128
+STEP_SPLITS = {
+    (0, 0): [(0, 0, 0, 2), (0, 0, 2, 2)],
+    (1, 6): [(1, 6, 0, 2), (1, 7, 0, 2), (1, 6, 2, 2)],
+    (1, 7): [(1, 7, 2, 1), (1, 7, 3, 1)],
+}
+VECTOR_EMPTIES = 2
 RUN = 4
 
 FLOPS = 2 * L2 * KC * TOKENS
@@ -63,8 +69,8 @@ def tile_bhcn_awx_pa_t_v_kernel(tc, mid_logits, x, W2, b2, rstd, p, grad_out, ou
         c_in = ctx.enter_context(tc.tile_pool(name="c_in", bufs=3))
         small = ctx.enter_context(tc.tile_pool(name="small", bufs=3))
         c_grouped_pool = ctx.enter_context(tc.tile_pool(name="c_grouped_pool", bufs=2))
-        d_grouped_pool = ctx.enter_context(tc.tile_pool(name="d_grouped_pool", bufs=2 * CHUNKS))
-        d_pool = ctx.enter_context(tc.tile_pool(name="d_pool", bufs=3 * CHUNKS))
+        d_grouped_pool = ctx.enter_context(tc.tile_pool(name="d_grouped_pool", bufs=3))
+        d_pool = ctx.enter_context(tc.tile_pool(name="d_pool", bufs=4))
         out_pool = ctx.enter_context(tc.tile_pool(name="out_pool", bufs=M_TILES))
         psum = ctx.enter_context(tc.psum_pool(name="psum", bufs=1))
         ctx.enter_context(tc.manual_schedule(engines={mybir.EngineType.SP}))
@@ -154,63 +160,84 @@ def tile_bhcn_awx_pa_t_v_kernel(tc, mid_logits, x, W2, b2, rstd, p, grad_out, ou
             nc.gpsimd.tensor_tensor(out=row_sum[c][:], in0=fold_sum[:], in1=rest_sum[:], op=ALU.add)
         quantise_c(*waiting)
 
+        items = []
         for r in range(ROUNDS):
-            d_cols = slice(r * ROUND_COLS, (r + 1) * ROUND_COLS)
-            acc = [
-                [psum.tile([P, N_TILE], F32, name="acc%d%d" % (m, n)) for n in range(N_TILES)]
-                for m in range(M_TILES)
-            ]
-
             for c in range(PASSES):
-                p_sb = p_pool.tile([P, PACK, ROUND_COLS], F32)
-                nc.sync.dma_start(out=p_sb[:], in_=p_v[c, :, :, d_cols])
+                items.extend(STEP_SPLITS.get((r, c), [(r, c, 0, M_TILES)]))
 
+        scaled_p = {}
+        acc = {}
+
+        def grouped_dli(r, c, m0, tiles):
+            if (r, c) not in scaled_p:
+                p_sb = p_pool.tile([P, PACK, ROUND_COLS], F32)
+                nc.sync.dma_start(out=p_sb[:], in_=p_v[c, :, :, r * ROUND_COLS : (r + 1) * ROUND_COLS])
                 for t in range(PACK):
                     nc.scalar.activation(
                         out=p_sb[:, t, :], in_=p_sb[:, t, :], func=ACT.Copy,
                         scale=row_sum[c][:, t : t + 1],
                     )
+                scaled_p[(r, c)] = p_sb
+            col0 = m0 * M_TILE
+            cols = tiles * M_TILE
+            d_grouped = d_grouped_pool.tile([P, cols, PACK], BF16, align_bytes=64)
+            nc.vector.tensor_tensor(
+                out=as_grouped(d_grouped[:]),
+                in0=as_rows(g_sb[c][:, :, r * ROUND_COLS + col0 : r * ROUND_COLS + col0 + cols]),
+                in1=as_rows(scaled_p[(r, c)][:, :, col0 : col0 + cols]),
+                op=ALU.subtract,
+            )
+            return d_grouped
 
-                d_grouped = []
-                for k in range(CHUNKS):
-                    p_col0 = k * CHUNK_COLS
-                    g_col0 = r * ROUND_COLS + p_col0
-                    d_grouped.append(
-                        d_grouped_pool.tile([P, CHUNK_COLS, PACK], BF16, name="d_grouped", align_bytes=64)
-                    )
-                    nc.vector.tensor_tensor(
-                        out=as_grouped(d_grouped[k][:]),
-                        in0=as_rows(g_sb[c][:, :, g_col0 : g_col0 + CHUNK_COLS]),
-                        in1=as_rows(p_sb[:, :, p_col0 : p_col0 + CHUNK_COLS]),
-                        op=ALU.subtract,
+        def multiply(c, m0, tiles, d_grouped):
+            d_codes = d_pool.tile([P, tiles * M_TILE], U32, align_bytes=64)
+            d_scales = d_pool.tile([P, tiles * M_TILE], U8, align_bytes=64)
+            nc.vector.quantize_mx(
+                out=d_codes[:].bitcast(E5M2_X4),
+                scales=d_scales[:],
+                in_=d_grouped[:].rearrange("q w t -> q (w t)"),
+            )
+            for i in range(tiles):
+                m_cols = slice(i * M_TILE, (i + 1) * M_TILE)
+                for n in range(N_TILES):
+                    n_cols = slice(n * N_TILE, (n + 1) * N_TILE)
+                    if c == 0:
+                        acc[(m0 + i, n)] = psum.tile([P, N_TILE], F32, name="acc%d%d" % (m0 + i, n))
+                    nc.tensor.matmul_mx(
+                        out=acc[(m0 + i, n)][:],
+                        lhsT=d_codes[:, m_cols].bitcast(E5M2_X4),
+                        lhsT_scale=d_scales[:, m_cols],
+                        rhs=c_codes[c][:, n_cols].bitcast(E4M3_X4),
+                        rhs_scale=c_scales[c][:, n_cols],
+                        start=(c == 0),
+                        stop=(c == PASSES - 1),
                     )
 
-                for k in range(CHUNKS):
-                    d_codes = d_pool.tile([P, CHUNK_COLS], U32, align_bytes=64)
-                    d_scales = d_pool.tile([P, CHUNK_COLS], U8, align_bytes=64)
-                    nc.vector.quantize_mx(
-                        out=d_codes[:].bitcast(E5M2_X4),
-                        scales=d_scales[:],
-                        in_=d_grouped[k][:].rearrange("q w t -> q (w t)"),
-                    )
-                    for i in range(CHUNK_TILES):
-                        m_cols = slice(i * M_TILE, (i + 1) * M_TILE)
-                        for n in range(N_TILES):
-                            n_cols = slice(n * N_TILE, (n + 1) * N_TILE)
-                            nc.tensor.matmul_mx(
-                                out=acc[k * CHUNK_TILES + i][n][:],
-                                lhsT=d_codes[:, m_cols].bitcast(E5M2_X4),
-                                lhsT_scale=d_scales[:, m_cols],
-                                rhs=c_codes[c][:, n_cols].bitcast(E4M3_X4),
-                                rhs_scale=c_scales[c][:, n_cols],
-                                start=(c == 0),
-                                stop=(c == PASSES - 1),
-                            )
+        def empty(r, m, with_vector):
+            rows = slice(r * ROUND_COLS + m * M_TILE, r * ROUND_COLS + (m + 1) * M_TILE)
+            staged = out_pool.tile([P, KC], F32)
+            nc.scalar.copy(out=staged[:, 0:N_TILE], in_=acc[(m, 0)][:])
+            if with_vector:
+                nc.vector.tensor_copy(out=staged[:, N_TILE:KC], in_=acc[(m, 1)][:])
+                nc.scalar.dma_start(out=out[rows, 0:N_TILE], in_=staged[:, 0:N_TILE])
+                nc.sync.dma_start(out=out[rows, N_TILE:KC], in_=staged[:, N_TILE:KC])
+            else:
+                nc.scalar.copy(out=staged[:, N_TILE:KC], in_=acc[(m, 1)][:])
+                nc.scalar.dma_start(out=out[rows, :], in_=staged[:])
 
-            for m in range(M_TILES):
-                row0 = r * ROUND_COLS + m * M_TILE
-                staged = out_pool.tile([P, KC], F32)
-                nc.scalar.copy(out=staged[:, 0:N_TILE], in_=acc[m][0][:])
-                second_copy = nc.vector.tensor_copy if r == ROUNDS - 1 else nc.scalar.copy
-                second_copy(out=staged[:, N_TILE:KC], in_=acc[m][1][:])
-                nc.scalar.dma_start(out=out[row0 : row0 + M_TILE, :], in_=staged[:])
+        grouped = {}
+        shared = []
+        for k in range(len(items) + 1):
+            if k < len(items):
+                grouped[k] = grouped_dli(*items[k])
+            if k > 0:
+                r, c, m0, tiles = items[k - 1]
+                multiply(c, m0, tiles, grouped[k - 1])
+                if c == PASSES - 1:
+                    for m in range(m0, m0 + tiles):
+                        if r == ROUNDS - 1 and m >= M_TILES - VECTOR_EMPTIES:
+                            shared.append((r, m))
+                        else:
+                            empty(r, m, False)
+        for r, m in shared:
+            empty(r, m, True)

@@ -39,8 +39,9 @@ STEP_SPLITS = {
     (1, 6): [(1, 6, 0, 2), (1, 7, 0, 2), (1, 6, 2, 2)],
     (1, 7): [(1, 7, 2, 1), (1, 7, 3, 1)],
 }
+PIECEWISE_P = [(0, 0)]
 VECTOR_EMPTIES = 2
-RUN = 4
+RUN = 8
 
 FLOPS = 2 * L2 * KC * TOKENS
 BYTES = TOKENS * (2 * D_HN + 2 * D_X + 4 + 4 * L2 + 2 * L2) + 4 * L2 * KC
@@ -171,12 +172,19 @@ def tile_bhcn_awx_pa_t_v_kernel(tc, mid_logits, x, W2, b2, rstd, p, grad_out, ou
         def grouped_dli(r, c, m0, tiles):
             if (r, c) not in scaled_p:
                 p_sb = p_pool.tile([P, PACK, ROUND_COLS], F32)
-                nc.sync.dma_start(out=p_sb[:], in_=p_v[c, :, :, r * ROUND_COLS : (r + 1) * ROUND_COLS])
-                for t in range(PACK):
-                    nc.scalar.activation(
-                        out=p_sb[:, t, :], in_=p_sb[:, t, :], func=ACT.Copy,
-                        scale=row_sum[c][:, t : t + 1],
+                pieces = len(STEP_SPLITS[(r, c)]) if (r, c) in PIECEWISE_P else 1
+                width = ROUND_COLS // pieces
+                for i in range(pieces):
+                    piece = slice(i * width, (i + 1) * width)
+                    nc.sync.dma_start(
+                        out=p_sb[:, :, piece],
+                        in_=p_v[c, :, :, r * ROUND_COLS + i * width : r * ROUND_COLS + (i + 1) * width],
                     )
+                    for t in range(PACK):
+                        nc.scalar.activation(
+                            out=p_sb[:, t, piece], in_=p_sb[:, t, piece], func=ACT.Copy,
+                            scale=row_sum[c][:, t : t + 1],
+                        )
                 scaled_p[(r, c)] = p_sb
             col0 = m0 * M_TILE
             cols = tiles * M_TILE

@@ -94,20 +94,29 @@ def tile_bhcn_awx_pa_t_v_kernel(tc, mid_logits, x, W2, b2, rstd, p, grad_out, ou
             )
 
         waiting = None
-        for c in range(PASSES):
+        c_tiles = {}
+
+        def fetch_c(c):
             mid_sb = c_in.tile([P, PACK, D_HN], BF16)
             x_sb = c_in.tile([P, PACK, D_X], BF16)
-            x_pieces = 2 if c == 0 else 1
-            x_cols = D_X // x_pieces
             if c == 0:
-                for i in range(x_pieces):
-                    for t in range(i * PACK // x_pieces, (i + 1) * PACK // x_pieces):
+                for i in range(2):
+                    for t in range(i * PACK // 2, (i + 1) * PACK // 2):
                         nc.sync.dma_start(out=mid_sb[:, t, :], in_=mid_v[c, :, t, :])
-                    piece = slice(i * x_cols, (i + 1) * x_cols)
+                    piece = slice(i * D_X // 2, (i + 1) * D_X // 2)
                     nc.sync.dma_start(out=x_sb[:, :, piece], in_=x_v[c, :, :, piece])
             else:
                 nc.sync.dma_start(out=mid_sb[:], in_=mid_v[c])
                 nc.sync.dma_start(out=x_sb[:], in_=x_v[c])
+            c_tiles[c] = (mid_sb, x_sb)
+
+        fetch_c(0)
+        for c in range(PASSES):
+            if c + 1 < PASSES:
+                fetch_c(c + 1)
+            mid_sb, x_sb = c_tiles[c]
+            x_pieces = 2 if c == 0 else 1
+            x_cols = D_X // x_pieces
             nc.sync.dma_start(out=g_sb[c][:], in_=g_v[c])
 
             h_sum = small.tile([P, PACK], F32)

@@ -111,9 +111,10 @@ def tile_bhcn_awx_pa_t_v_kernel(tc, mid_logits, x, W2, b2, rstd, p, grad_out, ou
             c_tiles[c] = (mid_sb, x_sb)
 
         fetch_c(0)
+        fetch_c(1)
         for c in range(PASSES):
-            if c + 1 < PASSES:
-                fetch_c(c + 1)
+            if c + 2 < PASSES:
+                fetch_c(c + 2)
             mid_sb, x_sb = c_tiles[c]
             x_pieces = 2 if c == 0 else 1
             x_cols = D_X // x_pieces

@@ -36,8 +36,10 @@ FOLD_COLS = 800
 SCALAR_X_COLS = 128
 STEP_SPLITS = {
     (0, 0): [(0, 0, 0, 2), (0, 0, 2, 2)],
-    (1, 6): [(1, 6, 0, 2), (1, 7, 0, 2), (1, 6, 2, 2)],
-    (1, 7): [(1, 7, 2, 1), (1, 7, 3, 1)],
+    (1, 4): [(1, 4, 0, 3)],
+    (1, 5): [(1, 5, 0, 3)],
+    (1, 6): [(1, 6, 0, 2)],
+    (1, 7): [(1, 7, 0, 2), (1, 6, 2, 2), (1, 4, 3, 1), (1, 5, 3, 1), (1, 7, 2, 1), (1, 7, 3, 1)],
 }
 PIECEWISE_P = [(0, 0)]
 VECTOR_EMPTIES = 2
@@ -210,11 +212,15 @@ def tile_bhcn_awx_pa_t_v_kernel(tc, mid_logits, x, W2, b2, rstd, p, grad_out, ou
         def multiply(c, m0, tiles, d_grouped):
             d_codes = d_pool.tile([P, tiles * M_TILE], U32, align_bytes=64)
             d_scales = d_pool.tile([P, tiles * M_TILE], U8, align_bytes=64)
-            nc.vector.quantize_mx(
-                out=d_codes[:].bitcast(E5M2_X4),
-                scales=d_scales[:],
-                in_=d_grouped[:].rearrange("q w t -> q (w t)"),
-            )
+            first = 0
+            for part in ([2, 1] if tiles == 3 else [tiles]):
+                q_cols = slice(first * M_TILE, (first + part) * M_TILE)
+                nc.vector.quantize_mx(
+                    out=d_codes[:, q_cols].bitcast(E5M2_X4),
+                    scales=d_scales[:, q_cols],
+                    in_=d_grouped[:, q_cols, :].rearrange("q w t -> q (w t)"),
+                )
+                first += part
             for i in range(tiles):
                 m_cols = slice(i * M_TILE, (i + 1) * M_TILE)
                 for n in range(N_TILES):

from contextlib import ExitStack

import concourse.mybir as mybir
from concourse.masks import make_identity

F32 = mybir.dt.float32
BF16 = mybir.dt.bfloat16
U32 = mybir.dt.uint32
U8 = mybir.dt.uint8
E4M3_X4 = mybir.dt.float8_e4m3fn_x4
E5M2_X4 = mybir.dt.float8_e5m2_x4
ALU = mybir.AluOpType
ACT = mybir.ActivationFunctionType
AX = mybir.AxisListType

P = 128
PACK = 4
TOKENS = 4096
PASSES = TOKENS // (P * PACK)
D_HN = 512
D_X = 512
KC = D_HN + D_X
L2 = 1024
M_TILE = 128
N_TILE = 512
N_TILES = KC // N_TILE
PSUM_BANKS = 8
M_TILES = PSUM_BANKS // N_TILES
ROUND_COLS = M_TILES * M_TILE
ROUNDS = L2 // ROUND_COLS
CHUNK_TILES = 2
CHUNK_COLS = CHUNK_TILES * M_TILE
CHUNKS = M_TILES // CHUNK_TILES
FOLD_W = 32
FOLD_COLS = 800
SCALAR_X_COLS = 128
STEP_SPLITS = {
    (0, 0): [(0, 0, 0, 2), (0, 0, 2, 2)],
    (1, 4): [(1, 4, 0, 3)],
    (1, 5): [(1, 5, 0, 3)],
    (1, 6): [(1, 6, 0, 2)],
    (1, 7): [(1, 7, 0, 2), (1, 6, 2, 2), (1, 4, 3, 1), (1, 5, 3, 1), (1, 7, 2, 1), (1, 7, 3, 1)],
}
PIECEWISE_P = [(0, 0)]
VECTOR_EMPTIES = 2
RUN = 8

FLOPS = 2 * L2 * KC * TOKENS
BYTES = TOKENS * (2 * D_HN + 2 * D_X + 4 + 4 * L2 + 2 * L2) + 4 * L2 * KC


def as_rows(rows):
    return rows.rearrange("q t (b i) -> q b t i", i=RUN)


def as_grouped(grouped):
    return grouped.rearrange("q (b i) t -> q b t i", i=RUN)


def tile_bhcn_awx_pa_t_v_kernel(tc, mid_logits, x, W2, b2, rstd, p, grad_out, out):
    nc = tc.nc

    mid_v = mid_logits.rearrange("(c q t) w -> c q t w", q=P, t=PACK)
    x_v = x.rearrange("(c q t) w -> c q t w", q=P, t=PACK)
    p_v = p.rearrange("(c q t) w -> c q t w", q=P, t=PACK)
    g_v = grad_out.rearrange("(c q t) w -> c q t w", q=P, t=PACK)
    rstd_v = rstd.rearrange("(c q t) o -> q c (t o)", q=P, t=PACK)

    with ExitStack() as ctx:
        keep = ctx.enter_context(tc.tile_pool(name="keep", bufs=1))
        p_pool = ctx.enter_context(tc.tile_pool(name="p_pool", bufs=6))
        c_in = ctx.enter_context(tc.tile_pool(name="c_in", bufs=3))
        small = ctx.enter_context(tc.tile_pool(name="small", bufs=3))
        c_grouped_pool = ctx.enter_context(tc.tile_pool(name="c_grouped_pool", bufs=2))
        d_grouped_pool = ctx.enter_context(tc.tile_pool(name="d_grouped_pool", bufs=3))
        d_pool = ctx.enter_context(tc.tile_pool(name="d_pool", bufs=4))
        out_pool = ctx.enter_context(tc.tile_pool(name="out_pool", bufs=M_TILES))
        psum = ctx.enter_context(tc.psum_pool(name="psum", bufs=1))
        ctx.enter_context(tc.manual_schedule(engines={mybir.EngineType.SP}))

        rstd_sb = keep.tile([P, PASSES, PACK], F32)
        ident = keep.tile([P, P], BF16)
        g_sb = [keep.tile([P, PACK, L2], BF16, name="g_sb%d" % c) for c in range(PASSES)]
        row_sum = [keep.tile([P, PACK], F32, name="row_sum%d" % c) for c in range(PASSES)]
        c_codes = [keep.tile([P, KC], U32, name="c_codes%d" % c, align_bytes=64) for c in range(PASSES)]
        c_scales = [keep.tile([P, KC], U8, name="c_scales%d" % c, align_bytes=64) for c in range(PASSES)]

        nc.scalar.dma_start(out=rstd_sb[:], in_=rstd_v)
        make_identity(nc, ident[:])

        def quantise_c(c, c_grouped):
            nc.vector.quantize_mx(
                out=c_codes[c][:].bitcast(E4M3_X4),
                scales=c_scales[c][:],
                in_=c_grouped[:].rearrange("q w t -> q (w t)"),
            )

        waiting = None
        c_tiles = {}

        def fetch_c(c):
            mid_sb = c_in.tile([P, PACK, D_HN], BF16)
            x_sb = c_in.tile([P, PACK, D_X], BF16)
            if c == 0:
                for i in range(2):
                    for t in range(i * PACK // 2, (i + 1) * PACK // 2):
                        nc.sync.dma_start(out=mid_sb[:, t, :], in_=mid_v[c, :, t, :])
                    piece = slice(i * D_X // 2, (i + 1) * D_X // 2)
                    nc.sync.dma_start(out=x_sb[:, :, piece], in_=x_v[c, :, :, piece])
            else:
                nc.sync.dma_start(out=mid_sb[:], in_=mid_v[c])
                nc.sync.dma_start(out=x_sb[:], in_=x_v[c])
            c_tiles[c] = (mid_sb, x_sb)

        fetch_c(0)
        fetch_c(1)
        for c in range(PASSES):
            if c + 2 < PASSES:
                fetch_c(c + 2)
            mid_sb, x_sb = c_tiles[c]
            x_pieces = 2 if c == 0 else 1
            x_cols = D_X // x_pieces
            nc.sync.dma_start(out=g_sb[c][:], in_=g_v[c])

            h_sum = small.tile([P, PACK], F32)
            for t in range(PACK):
                nc.scalar.activation(
                    out=mid_sb[:, t, :], in_=mid_sb[:, t, :], func=ACT.Relu,
                    accum_out=h_sum[:, t : t + 1],
                )
            mu = small.tile([P, PACK], F32)
            nc.scalar.mul(mu[:], h_sum[:], 1.0 / D_HN)
            rest_sum = small.tile([P, PACK], F32)
            unused = small.tile([P, L2 - FOLD_COLS], BF16)
            for t in range(PACK):
                nc.scalar.activation(
                    out=unused[:], in_=g_sb[c][:, t, FOLD_COLS:L2], func=ACT.Copy,
                    accum_out=rest_sum[:, t : t + 1],
                )

            bank = psum.tile([P, N_TILE], F32, name="acc%d%d" % (c // N_TILES, c % N_TILES))
            fold = bank[:, 0 : PACK * FOLD_W].rearrange("q (t i) -> q t i", t=PACK)
            folds = FOLD_COLS // FOLD_W
            for j in range(folds):
                nc.tensor.matmul(
                    out=fold, lhsT=ident[:], rhs=g_sb[c][:, :, j * FOLD_W : (j + 1) * FOLD_W],
                    start=(j == 0), stop=(j == folds - 1),
                )

            c_grouped = c_grouped_pool.tile([P, KC, PACK], BF16, align_bytes=64)
            nc.scalar.copy(
                out=as_grouped(c_grouped[:, KC - SCALAR_X_COLS : KC, :]),
                in_=as_rows(x_sb[:, :, D_X - SCALAR_X_COLS : D_X]),
            )
            for i in range(x_pieces):
                last = min((i + 1) * x_cols, D_X - SCALAR_X_COLS)
                nc.vector.tensor_copy(
                    out=as_grouped(c_grouped[:, D_HN + i * x_cols : D_HN + last, :]),
                    in_=as_rows(x_sb[:, :, i * x_cols : last]),
                )
            if waiting is not None:
                quantise_c(*waiting)
            for t in range(PACK):
                nc.vector.tensor_scalar(
                    out=mid_sb[:, t, :], in0=mid_sb[:, t, :],
                    scalar1=mu[:, t : t + 1], scalar2=rstd_sb[:, c, t : t + 1],
                    op0=ALU.subtract, op1=ALU.mult,
                )
            nc.vector.tensor_copy(out=as_grouped(c_grouped[:, 0:D_HN, :]), in_=as_rows(mid_sb[:]))
            waiting = (c, c_grouped)
            fold_sum = small.tile([P, PACK], F32)
            nc.vector.tensor_reduce(out=fold_sum[:], in_=fold, axis=AX.X, op=ALU.add)
            nc.gpsimd.tensor_tensor(out=row_sum[c][:], in0=fold_sum[:], in1=rest_sum[:], op=ALU.add)
        quantise_c(*waiting)

        items = []
        for r in range(ROUNDS):
            for c in range(PASSES):
                items.extend(STEP_SPLITS.get((r, c), [(r, c, 0, M_TILES)]))

        scaled_p = {}
        acc = {}

        def grouped_dli(r, c, m0, tiles):
            if (r, c) not in scaled_p:
                p_sb = p_pool.tile([P, PACK, ROUND_COLS], F32)
                pieces = len(STEP_SPLITS[(r, c)]) if (r, c) in PIECEWISE_P else 1
                width = ROUND_COLS // pieces
                for i in range(pieces):
                    piece = slice(i * width, (i + 1) * width)
                    nc.sync.dma_start(
                        out=p_sb[:, :, piece],
                        in_=p_v[c, :, :, r * ROUND_COLS + i * width : r * ROUND_COLS + (i + 1) * width],
                    )
                    for t in range(PACK):
                        nc.scalar.activation(
                            out=p_sb[:, t, piece], in_=p_sb[:, t, piece], func=ACT.Copy,
                            scale=row_sum[c][:, t : t + 1],
                        )
                scaled_p[(r, c)] = p_sb
            col0 = m0 * M_TILE
            cols = tiles * M_TILE
            d_grouped = d_grouped_pool.tile([P, cols, PACK], BF16, align_bytes=64)
            nc.vector.tensor_tensor(
                out=as_grouped(d_grouped[:]),
                in0=as_rows(g_sb[c][:, :, r * ROUND_COLS + col0 : r * ROUND_COLS + col0 + cols]),
                in1=as_rows(scaled_p[(r, c)][:, :, col0 : col0 + cols]),
                op=ALU.subtract,
            )
            return d_grouped

        def multiply(c, m0, tiles, d_grouped):
            d_codes = d_pool.tile([P, tiles * M_TILE], U32, align_bytes=64)
            d_scales = d_pool.tile([P, tiles * M_TILE], U8, align_bytes=64)
            first = 0
            for part in ([2, 1] if tiles == 3 else [tiles]):
                q_cols = slice(first * M_TILE, (first + part) * M_TILE)
                nc.vector.quantize_mx(
                    out=d_codes[:, q_cols].bitcast(E5M2_X4),
                    scales=d_scales[:, q_cols],
                    in_=d_grouped[:, q_cols, :].rearrange("q w t -> q (w t)"),
                )
                first += part
            for i in range(tiles):
                m_cols = slice(i * M_TILE, (i + 1) * M_TILE)
                for n in range(N_TILES):
                    n_cols = slice(n * N_TILE, (n + 1) * N_TILE)
                    if c == 0:
                        acc[(m0 + i, n)] = psum.tile([P, N_TILE], F32, name="acc%d%d" % (m0 + i, n))
                    nc.tensor.matmul_mx(
                        out=acc[(m0 + i, n)][:],
                        lhsT=d_codes[:, m_cols].bitcast(E5M2_X4),
                        lhsT_scale=d_scales[:, m_cols],
                        rhs=c_codes[c][:, n_cols].bitcast(E4M3_X4),
                        rhs_scale=c_scales[c][:, n_cols],
                        start=(c == 0),
                        stop=(c == PASSES - 1),
                    )

        def empty(r, m, with_vector):
            rows = slice(r * ROUND_COLS + m * M_TILE, r * ROUND_COLS + (m + 1) * M_TILE)
            staged = out_pool.tile([P, KC], F32)
            nc.scalar.copy(out=staged[:, 0:N_TILE], in_=acc[(m, 0)][:])
            if with_vector:
                nc.vector.tensor_copy(out=staged[:, N_TILE:KC], in_=acc[(m, 1)][:])
                nc.scalar.dma_start(out=out[rows, 0:N_TILE], in_=staged[:, 0:N_TILE])
                nc.sync.dma_start(out=out[rows, N_TILE:KC], in_=staged[:, N_TILE:KC])
            else:
                nc.scalar.copy(out=staged[:, N_TILE:KC], in_=acc[(m, 1)][:])
                nc.scalar.dma_start(out=out[rows, :], in_=staged[:])

        grouped = {}
        shared = []
        for k in range(len(items) + 1):
            if k < len(items):
                grouped[k] = grouped_dli(*items[k])
            if k > 0:
                r, c, m0, tiles = items[k - 1]
                multiply(c, m0, tiles, grouped[k - 1])
                if c == PASSES - 1:
                    for m in range(m0, m0 + tiles):
                        if r == ROUNDS - 1 and m >= M_TILES - VECTOR_EMPTIES:
                            shared.append((r, m))
                        else:
                            empty(r, m, False)
        for r, m in shared:
            empty(r, m, True)
